import numpy as np
import ml_dtypes


def mxq(x, axis, fmt="e4m3"):
    dtype, down = {"e4m3": (ml_dtypes.float8_e4m3fn, 7), "e5m2": (ml_dtypes.float8_e5m2, 14)}[fmt]
    v = np.moveaxis(np.asarray(x, np.float32).astype(ml_dtypes.bfloat16).astype(np.float64), axis, -1)
    blocks = v.reshape(v.shape[:-1] + (-1, 32))
    amax = np.abs(blocks).max(-1, keepdims=True)
    byte = np.maximum(np.where(amax > 0, np.frexp(amax)[1] - 1 + 127, 0) - down, 1)
    scale = np.exp2(byte - 127.0)
    codes = (blocks / scale).astype(np.float32).astype(dtype).astype(np.float64)
    return np.moveaxis((codes * scale).reshape(v.shape), -1, axis)


WIDE = False


def mx_kscale(k):
    if not WIDE:
        return np.ones(k)
    levels = np.array([10, -10, 5, -5, 0])
    a = np.random.permutation(np.resize(levels, k // 512 * 4)).reshape(k // 512, 4)
    idx = np.arange(k)
    return np.exp2(a[idx // 512, idx % 128 // 32])


BF16 = ml_dtypes.bfloat16


def bf(x):
    return np.asarray(x, np.float32).astype(BF16)


def f64(x):
    return np.asarray(x).astype(np.float64)


B, S, DIM, HEADS, DH = 1, 128, 512, 4, 128
HD = HEADS * DH
LN_EPS = 1e-5


def setup_inputs():
    s, t = mx_kscale(DIM), mx_kscale(HD)
    return {
        "x": bf(np.random.standard_normal((S, DIM)) + 0.5),
        "ln_w": bf((1.0 + 0.1 * np.random.standard_normal(DIM)) * s),
        "ln_b": bf(0.1 * np.random.standard_normal(DIM) * s),
        "W_c": bf(np.random.standard_normal((HD, DIM)) / np.sqrt(DIM) / s * t[:, None]),
        "b_c": bf(0.1 * np.random.standard_normal(HD) * t),
        "W_K": bf(np.random.standard_normal((HEADS, DH, DH, DH)) * 0.5 / np.sqrt(HD) / t.reshape(HEADS, 1, 1, DH)),
    }


def reference(x, ln_w, ln_b, W_c, b_c, W_K):
    x = f64(x)
    mu = x.mean(-1, keepdims=True)
    var = x.var(-1, keepdims=True)
    xn = (x - mu) / np.sqrt(var + LN_EPS) * f64(ln_w) + f64(ln_b)
    c = (mxq(xn, 1, "e4m3") @ mxq(f64(W_c), 1, "e4m3").T) + f64(b_c)
    wk = f64(W_K).transpose(0, 3, 1, 2).reshape(HD, DH * DH)
    return (mxq(c, 1, "e4m3") @ mxq(wk, 0, "e4m3")).reshape(S, DH, DH)

@@ -1,0 +1,216 @@
+from contextlib import ExitStack
+
+import concourse.mybir as mybir
+from concourse.masks import make_identity
+
+F32 = mybir.dt.float32
+BF16 = mybir.dt.bfloat16
+U32 = mybir.dt.uint32
+U8 = mybir.dt.uint8
+FP8X4 = mybir.dt.float8_e4m3fn_x4
+ALU = mybir.AluOpType
+ACT = mybir.ActivationFunctionType
+
+P = 128
+PACK = 4
+DIM = 512
+HEADS = 4
+DH = 128
+COLS = DH * DH
+LN_EPS = 1e-5
+
+GROUPS = P // HEADS
+CHUNK_M = 32
+CHUNK_COLS = GROUPS * CHUNK_M
+CHUNKS = COLS // CHUNK_COLS
+PASS_COLS = 512
+PASS_M = PASS_COLS // GROUPS
+PASSES_PER_CHUNK = CHUNK_COLS // PASS_COLS
+PASSES = CHUNKS * PASSES_PER_CHUNK
+BANK_T = 4
+ROUND = 2
+
+FLOPS = 2 * P * DIM * HEADS * DH + 2 * P * HEADS * DH * COLS
+
+
+def tile_trittentioncube_pa_kernel(tc, x, ln_w, ln_b, W_c, b_c, W_K, out):
+    nc = tc.nc
+    wk_chunks = W_K.rearrange("n i j k -> n (i j k)").rearrange(
+        "n (c g row) -> n c g row", c=CHUNKS, g=GROUPS
+    )
+    out_cols = out.rearrange("r i j -> r (i j)")
+
+    with ExitStack() as ctx:
+        ctx.enter_context(tc.manual_schedule())
+        keep = ctx.enter_context(tc.tile_pool(name="keep", bufs=1))
+        raw_pool = ctx.enter_context(tc.tile_pool(name="raw", bufs=CHUNKS))
+        grouped_pool = ctx.enter_context(tc.tile_pool(name="grouped", bufs=4))
+        mx_pool = ctx.enter_context(tc.tile_pool(name="mx", bufs=6))
+        result_pool = ctx.enter_context(tc.tile_pool(name="result", bufs=10))
+        flip_psum = ctx.enter_context(tc.psum_pool(name="flip_psum", bufs=6))
+        sum_psum = ctx.enter_context(tc.psum_pool(name="sum_psum", bufs=2))
+
+        ident_bf = keep.tile([P, P], BF16)
+        make_identity(nc, ident_bf[:])
+        ident_f32 = keep.tile([P, P], F32)
+        make_identity(nc, ident_f32[:])
+        eps = keep.tile([P, 1], F32)
+        nc.vector.memset(eps[:], LN_EPS)
+        vec_rows = keep.tile([P, P], BF16)
+        nc.vector.memset(vec_rows[:], 0.0)
+
+        x_sb = keep.tile([P, DIM], BF16)
+        nc.sync.dma_start(out=x_sb[:], in_=x)
+        for row, vec in enumerate((ln_w, ln_b, b_c)):
+            nc.scalar.dma_start(
+                out=vec_rows[row * PACK : (row + 1) * PACK, :],
+                in_=vec.rearrange("(t p) -> t p", p=P),
+            )
+        wc_raw = keep.tile([P, HEADS, DIM], BF16)
+        nc.sync.dma_start(out=wc_raw[:], in_=W_c.rearrange("(n k) d -> k n d", k=P))
+        raw_tiles = []
+        for c in range(CHUNKS):
+            raw = raw_pool.tile([P, CHUNK_M * DH], BF16)
+            for n in range(HEADS):
+                nc.sync.dma_start(out=raw[n:P:HEADS, :], in_=wk_chunks[n, c])
+            raw_tiles.append(raw)
+
+        warm = keep.tile([P, 1], F32)
+        nc.scalar.activation(out=warm[:], in_=eps[:], func=ACT.Sqrt)
+
+        stats = keep.tile([P, 6], F32)
+        nc.vector.bn_stats(out=stats[:], in_=x_sb[:])
+        mean_var = keep.tile([P, 2], F32)
+        nc.vector.bn_aggr(out=mean_var[:], in_=stats[:])
+        std = keep.tile([P, 1], F32)
+        nc.scalar.activation(out=std[:], in_=mean_var[:, 1:2], func=ACT.Sqrt, bias=eps[:])
+
+        vec_flip = flip_psum.tile([P, P], BF16, tag="flip")
+        nc.tensor.transpose(vec_flip[:], vec_rows[:], ident_bf[:])
+        vecs = keep.tile([P, 3 * PACK], F32)
+        nc.vector.tensor_copy(out=vecs[:], in_=vec_flip[:, 0 : 3 * PACK])
+        gain = vecs[:, 0:PACK]
+        shift = vecs[:, PACK : 2 * PACK]
+        bias = vecs[:, 2 * PACK : 3 * PACK]
+
+        rstd = keep.tile([P, 1], F32)
+        nc.vector.reciprocal(out=rstd[:], in_=std[:])
+        xhat = keep.tile([P, DIM], F32)
+        nc.vector.tensor_scalar(
+            out=xhat[:], in0=x_sb[:], scalar1=mean_var[:, 0:1], scalar2=rstd[:],
+            op0=ALU.subtract, op1=ALU.mult,
+        )
+
+        wc_grouped = keep.tile([P, HEADS, DH, PACK], BF16, align_bytes=64)
+        for n in range(HEADS):
+            wc_flip = flip_psum.tile([P, PACK, DH], BF16, tag="flip")
+            for t in range(PACK):
+                nc.tensor.transpose(wc_flip[:, t, :], wc_raw[:, n, t * P : (t + 1) * P], ident_bf[:])
+            nc.scalar.copy(out=wc_grouped[:, n], in_=wc_flip[:].rearrange("p t k -> p k t"))
+        wc_codes = keep.tile([P, HEADS * DH], U32, align_bytes=64)
+        wc_scales = keep.tile([P, HEADS * DH], U8, align_bytes=64)
+        nc.vector.quantize_mx(
+            out=wc_codes[:].bitcast(FP8X4), scales=wc_scales[:],
+            in_=wc_grouped[:].rearrange("p n k t -> p (n k t)"),
+        )
+
+        xhat_flip = flip_psum.tile([P, PACK, P], F32, tag="flip")
+        for t in range(PACK):
+            nc.tensor.transpose(xhat_flip[:, t, :], xhat[:, t * P : (t + 1) * P], ident_f32[:])
+        xn_grouped = keep.tile([P, P, PACK], BF16, align_bytes=64)
+        for t in range(PACK):
+            nc.vector.tensor_scalar(
+                out=xn_grouped[:, :, t], in0=xhat_flip[:, t, :],
+                scalar1=gain[:, t : t + 1], scalar2=shift[:, t : t + 1], op0=ALU.mult, op1=ALU.add,
+            )
+        xn_codes = keep.tile([P, P], U32, align_bytes=64)
+        xn_scales = keep.tile([P, P], U8, align_bytes=64)
+        nc.vector.quantize_mx(
+            out=xn_codes[:].bitcast(FP8X4), scales=xn_scales[:],
+            in_=xn_grouped[:].rearrange("p r t -> p (r t)"),
+        )
+
+        grouped_tiles = {}
+        mx_tiles = {}
+        result_tiles = {}
+
+        def flip_pass(s):
+            raw = raw_tiles[s // PASSES_PER_CHUNK]
+            first_m = (s % PASSES_PER_CHUNK) * PASS_M
+            grouped = grouped_pool.tile([P, PASS_M * P], BF16, align_bytes=64)
+            for b in range(PASS_M // BANK_T):
+                flip = flip_psum.tile([P, BANK_T * P], BF16, tag="flip")
+                for q in range(BANK_T):
+                    m = first_m + b * BANK_T + q
+                    nc.tensor.transpose(flip[:, q * P : (q + 1) * P], raw[:, m * DH : (m + 1) * DH], ident_bf[:])
+                nc.scalar.copy(
+                    out=grouped[:, b * BANK_T * P : (b + 1) * BANK_T * P].bitcast(F32), in_=flip[:].bitcast(F32)
+                )
+            grouped_tiles[s] = grouped
+
+        def quantise_pass(s):
+            codes = mx_pool.tile([P, PASS_COLS], U32, align_bytes=64)
+            scales = mx_pool.tile([P, PASS_COLS], U8, align_bytes=64)
+            nc.vector.quantize_mx(out=codes[:].bitcast(FP8X4), scales=scales[:], in_=grouped_tiles[s][:])
+            mx_tiles[s] = (codes, scales)
+
+        def multiply_pass(s):
+            codes, scales = mx_tiles[s]
+            sums = sum_psum.tile([P, PASS_COLS], F32, tag="sums")
+            nc.tensor.matmul_mx(
+                out=sums[:], lhsT=c_codes[:].bitcast(FP8X4), lhsT_scale=c_scales[:],
+                rhs=codes[:].bitcast(FP8X4), rhs_scale=scales[:], start=True, stop=True,
+            )
+            c, half = divmod(s, PASSES_PER_CHUNK)
+            if half == 0:
+                result = result_pool.tile([P, CHUNK_COLS], F32)
+                result_tiles[c] = result
+            result = result_tiles[c]
+            nc.vector.tensor_copy(
+                out=result[:].rearrange("r (g h m) -> r h g m", g=GROUPS, h=PASSES_PER_CHUNK)[:, half],
+                in_=sums[:].rearrange("r (m g) -> r g m", g=GROUPS),
+            )
+            if half == PASSES_PER_CHUNK - 1:
+                nc.sync.dma_start(out=out_cols[:, c * CHUNK_COLS : (c + 1) * CHUNK_COLS], in_=result[:])
+
+        def flip_round(i):
+            for s in range(i * ROUND, (i + 1) * ROUND):
+                flip_pass(s)
+
+        def quantise_round(i):
+            for s in range(i * ROUND, (i + 1) * ROUND):
+                quantise_pass(s)
+
+        def multiply_round(i):
+            for s in range(i * ROUND, (i + 1) * ROUND):
+                multiply_pass(s)
+
+        flip_round(0)
+        c_sums = sum_psum.tile([P, HEADS, P], F32, tag="sums")
+        for n in range(HEADS):
+            nc.tensor.matmul_mx(
+                out=c_sums[:, n, :],
+                lhsT=wc_codes[:, n * DH : (n + 1) * DH].bitcast(FP8X4),
+                lhsT_scale=wc_scales[:, n * DH : (n + 1) * DH],
+                rhs=xn_codes[:].bitcast(FP8X4), rhs_scale=xn_scales[:], start=True, stop=True,
+            )
+        quantise_round(0)
+        c_grouped = keep.tile([P, P, HEADS], BF16, align_bytes=64)
+        for n in range(HEADS):
+            nc.vector.tensor_scalar(
+                out=c_grouped[:, :, n], in0=c_sums[:, n, :],
+                scalar1=bias[:, n : n + 1], scalar2=None, op0=ALU.add,
+            )
+        c_codes = keep.tile([P, P], U32, align_bytes=64)
+        c_scales = keep.tile([P, P], U8, align_bytes=64)
+        nc.vector.quantize_mx(
+            out=c_codes[:].bitcast(FP8X4), scales=c_scales[:],
+            in_=c_grouped[:].rearrange("k r n -> k (r n)"),
+        )
+
+        rounds = PASSES // ROUND
+        for i in range(1, rounds):
+            flip_round(i)
+            quantise_round(i)
+            multiply_round(i - 1)
+        multiply_round(rounds - 1)

@@ -29,6 +29,7 @@ PASSES_PER_CHUNK = CHUNK_COLS // PASS_COLS
 PASSES = CHUNKS * PASSES_PER_CHUNK
 BANK_T = 4
 ROUND = 2
+LINE_F32 = 4
 
 FLOPS = 2 * P * DIM * HEADS * DH + 2 * P * HEADS * DH * COLS
 
@@ -44,9 +45,9 @@ def tile_trittentioncube_pa_kernel(tc, x, ln_w, ln_b, W_c, b_c, W_K, out):
         ctx.enter_context(tc.manual_schedule())
         keep = ctx.enter_context(tc.tile_pool(name="keep", bufs=1))
         raw_pool = ctx.enter_context(tc.tile_pool(name="raw", bufs=CHUNKS))
-        grouped_pool = ctx.enter_context(tc.tile_pool(name="grouped", bufs=4))
-        mx_pool = ctx.enter_context(tc.tile_pool(name="mx", bufs=6))
-        result_pool = ctx.enter_context(tc.tile_pool(name="result", bufs=10))
+        grouped_pool = ctx.enter_context(tc.tile_pool(name="grouped", bufs=3))
+        mx_pool = ctx.enter_context(tc.tile_pool(name="mx", bufs=4))
+        result_pool = ctx.enter_context(tc.tile_pool(name="result", bufs=CHUNKS))
         flip_psum = ctx.enter_context(tc.psum_pool(name="flip_psum", bufs=6))
         sum_psum = ctx.enter_context(tc.psum_pool(name="sum_psum", bufs=2))
 
@@ -167,8 +168,10 @@ def tile_trittentioncube_pa_kernel(tc, x, ln_w, ln_b, W_c, b_c, W_K, out):
                 result_tiles[c] = result
             result = result_tiles[c]
             nc.vector.tensor_copy(
-                out=result[:].rearrange("r (g h m) -> r h g m", g=GROUPS, h=PASSES_PER_CHUNK)[:, half],
-                in_=sums[:].rearrange("r (m g) -> r g m", g=GROUPS),
+                out=result[:].rearrange(
+                    "r (g h a b) -> r h a g b", g=GROUPS, h=PASSES_PER_CHUNK, b=LINE_F32
+                )[:, half],
+                in_=sums[:].rearrange("r (a b g) -> r a g b", b=LINE_F32, g=GROUPS),
             )
             if half == PASSES_PER_CHUNK - 1:
                 nc.sync.dma_start(out=out_cols[:, c * CHUNK_COLS : (c + 1) * CHUNK_COLS], in_=result[:])

@@ -30,6 +30,8 @@ PASSES = CHUNKS * PASSES_PER_CHUNK
 BANK_T = 4
 ROUND = 2
 LINE_F32 = 4
+WAIT_FOR_W_C = 8
+WAIT_FOR_W_K = 2
 
 FLOPS = 2 * P * DIM * HEADS * DH + 2 * P * HEADS * DH * COLS
 
@@ -51,6 +53,8 @@ def tile_trittentioncube_pa_kernel(tc, x, ln_w, ln_b, W_c, b_c, W_K, out):
         flip_psum = ctx.enter_context(tc.psum_pool(name="flip_psum", bufs=6))
         sum_psum = ctx.enter_context(tc.psum_pool(name="sum_psum", bufs=2))
 
+        zeros = keep.tile([P, PASS_COLS], BF16)
+        nc.vector.memset(zeros[:], 0.0)
         ident_bf = keep.tile([P, P], BF16)
         make_identity(nc, ident_bf[:])
         ident_f32 = keep.tile([P, P], F32)
@@ -63,7 +67,7 @@ def tile_trittentioncube_pa_kernel(tc, x, ln_w, ln_b, W_c, b_c, W_K, out):
         x_sb = keep.tile([P, DIM], BF16)
         nc.sync.dma_start(out=x_sb[:], in_=x)
         for row, vec in enumerate((ln_w, ln_b, b_c)):
-            nc.scalar.dma_start(
+            nc.sync.dma_start(
                 out=vec_rows[row * PACK : (row + 1) * PACK, :],
                 in_=vec.rearrange("(t p) -> t p", p=P),
             )
@@ -75,6 +79,15 @@ def tile_trittentioncube_pa_kernel(tc, x, ln_w, ln_b, W_c, b_c, W_K, out):
             for n in range(HEADS):
                 nc.sync.dma_start(out=raw[n:P:HEADS, :], in_=wk_chunks[n, c])
             raw_tiles.append(raw)
+
+        def raise_clock(count):
+            unread = sum_psum.tile([P, PASS_COLS], F32, tag="sums")
+            for i in range(count):
+                nc.tensor.matmul(
+                    out=unread[:], lhsT=zeros[:, 0:P], rhs=zeros[:], start=(i == 0), stop=(i == count - 1)
+                )
+
+        raise_clock(WAIT_FOR_W_C)
 
         warm = keep.tile([P, 1], F32)
         nc.scalar.activation(out=warm[:], in_=eps[:], func=ACT.Sqrt)
@@ -108,12 +121,6 @@ def tile_trittentioncube_pa_kernel(tc, x, ln_w, ln_b, W_c, b_c, W_K, out):
             for t in range(PACK):
                 nc.tensor.transpose(wc_flip[:, t, :], wc_raw[:, n, t * P : (t + 1) * P], ident_bf[:])
             nc.scalar.copy(out=wc_grouped[:, n], in_=wc_flip[:].rearrange("p t k -> p k t"))
-        wc_codes = keep.tile([P, HEADS * DH], U32, align_bytes=64)
-        wc_scales = keep.tile([P, HEADS * DH], U8, align_bytes=64)
-        nc.vector.quantize_mx(
-            out=wc_codes[:].bitcast(FP8X4), scales=wc_scales[:],
-            in_=wc_grouped[:].rearrange("p n k t -> p (n k t)"),
-        )
 
         xhat_flip = flip_psum.tile([P, PACK, P], F32, tag="flip")
         for t in range(PACK):
@@ -129,6 +136,12 @@ def tile_trittentioncube_pa_kernel(tc, x, ln_w, ln_b, W_c, b_c, W_K, out):
         nc.vector.quantize_mx(
             out=xn_codes[:].bitcast(FP8X4), scales=xn_scales[:],
             in_=xn_grouped[:].rearrange("p r t -> p (r t)"),
+        )
+        wc_codes = keep.tile([P, HEADS * DH], U32, align_bytes=64)
+        wc_scales = keep.tile([P, HEADS * DH], U8, align_bytes=64)
+        nc.vector.quantize_mx(
+            out=wc_codes[:].bitcast(FP8X4), scales=wc_scales[:],
+            in_=wc_grouped[:].rearrange("p n k t -> p (n k t)"),
         )
 
         grouped_tiles = {}
@@ -188,6 +201,7 @@ def tile_trittentioncube_pa_kernel(tc, x, ln_w, ln_b, W_c, b_c, W_K, out):
             for s in range(i * ROUND, (i + 1) * ROUND):
                 multiply_pass(s)
 
+        raise_clock(WAIT_FOR_W_K)
         flip_round(0)
         c_sums = sum_psum.tile([P, HEADS, P], F32, tag="sums")
         for n in range(HEADS):

from contextlib import ExitStack

import concourse.mybir as mybir
from concourse.masks import make_identity

F32 = mybir.dt.float32
BF16 = mybir.dt.bfloat16
U32 = mybir.dt.uint32
U8 = mybir.dt.uint8
FP8X4 = mybir.dt.float8_e4m3fn_x4
ALU = mybir.AluOpType
ACT = mybir.ActivationFunctionType

P = 128
PACK = 4
DIM = 512
HEADS = 4
DH = 128
COLS = DH * DH
LN_EPS = 1e-5

GROUPS = P // HEADS
CHUNK_M = 32
CHUNK_COLS = GROUPS * CHUNK_M
CHUNKS = COLS // CHUNK_COLS
PASS_COLS = 512
PASS_M = PASS_COLS // GROUPS
PASSES_PER_CHUNK = CHUNK_COLS // PASS_COLS
PASSES = CHUNKS * PASSES_PER_CHUNK
BANK_T = 4
ROUND = 2
LINE_F32 = 4
WAIT_FOR_W_C = 8
WAIT_FOR_W_K = 2

FLOPS = 2 * P * DIM * HEADS * DH + 2 * P * HEADS * DH * COLS


def tile_trittentioncube_pa_kernel(tc, x, ln_w, ln_b, W_c, b_c, W_K, out):
    nc = tc.nc
    wk_chunks = W_K.rearrange("n i j k -> n (i j k)").rearrange(
        "n (c g row) -> n c g row", c=CHUNKS, g=GROUPS
    )
    out_cols = out.rearrange("r i j -> r (i j)")

    with ExitStack() as ctx:
        ctx.enter_context(tc.manual_schedule())
        keep = ctx.enter_context(tc.tile_pool(name="keep", bufs=1))
        raw_pool = ctx.enter_context(tc.tile_pool(name="raw", bufs=CHUNKS))
        grouped_pool = ctx.enter_context(tc.tile_pool(name="grouped", bufs=3))
        mx_pool = ctx.enter_context(tc.tile_pool(name="mx", bufs=4))
        result_pool = ctx.enter_context(tc.tile_pool(name="result", bufs=CHUNKS))
        flip_psum = ctx.enter_context(tc.psum_pool(name="flip_psum", bufs=6))
        sum_psum = ctx.enter_context(tc.psum_pool(name="sum_psum", bufs=2))

        zeros = keep.tile([P, PASS_COLS], BF16)
        nc.vector.memset(zeros[:], 0.0)
        ident_bf = keep.tile([P, P], BF16)
        make_identity(nc, ident_bf[:])
        ident_f32 = keep.tile([P, P], F32)
        make_identity(nc, ident_f32[:])
        eps = keep.tile([P, 1], F32)
        nc.vector.memset(eps[:], LN_EPS)
        vec_rows = keep.tile([P, P], BF16)
        nc.vector.memset(vec_rows[:], 0.0)

        x_sb = keep.tile([P, DIM], BF16)
        nc.sync.dma_start(out=x_sb[:], in_=x)
        for row, vec in enumerate((ln_w, ln_b, b_c)):
            nc.sync.dma_start(
                out=vec_rows[row * PACK : (row + 1) * PACK, :],
                in_=vec.rearrange("(t p) -> t p", p=P),
            )
        wc_raw = keep.tile([P, HEADS, DIM], BF16)
        nc.sync.dma_start(out=wc_raw[:], in_=W_c.rearrange("(n k) d -> k n d", k=P))
        raw_tiles = []
        for c in range(CHUNKS):
            raw = raw_pool.tile([P, CHUNK_M * DH], BF16)
            for n in range(HEADS):
                nc.sync.dma_start(out=raw[n:P:HEADS, :], in_=wk_chunks[n, c])
            raw_tiles.append(raw)

        def raise_clock(count):
            unread = sum_psum.tile([P, PASS_COLS], F32, tag="sums")
            for i in range(count):
                nc.tensor.matmul(
                    out=unread[:], lhsT=zeros[:, 0:P], rhs=zeros[:], start=(i == 0), stop=(i == count - 1)
                )

        raise_clock(WAIT_FOR_W_C)

        warm = keep.tile([P, 1], F32)
        nc.scalar.activation(out=warm[:], in_=eps[:], func=ACT.Sqrt)

        stats = keep.tile([P, 6], F32)
        nc.vector.bn_stats(out=stats[:], in_=x_sb[:])
        mean_var = keep.tile([P, 2], F32)
        nc.vector.bn_aggr(out=mean_var[:], in_=stats[:])
        std = keep.tile([P, 1], F32)
        nc.scalar.activation(out=std[:], in_=mean_var[:, 1:2], func=ACT.Sqrt, bias=eps[:])

        vec_flip = flip_psum.tile([P, P], BF16, tag="flip")
        nc.tensor.transpose(vec_flip[:], vec_rows[:], ident_bf[:])
        vecs = keep.tile([P, 3 * PACK], F32)
        nc.vector.tensor_copy(out=vecs[:], in_=vec_flip[:, 0 : 3 * PACK])
        gain = vecs[:, 0:PACK]
        shift = vecs[:, PACK : 2 * PACK]
        bias = vecs[:, 2 * PACK : 3 * PACK]

        rstd = keep.tile([P, 1], F32)
        nc.vector.reciprocal(out=rstd[:], in_=std[:])
        xhat = keep.tile([P, DIM], F32)
        nc.vector.tensor_scalar(
            out=xhat[:], in0=x_sb[:], scalar1=mean_var[:, 0:1], scalar2=rstd[:],
            op0=ALU.subtract, op1=ALU.mult,
        )

        wc_grouped = keep.tile([P, HEADS, DH, PACK], BF16, align_bytes=64)
        for n in range(HEADS):
            wc_flip = flip_psum.tile([P, PACK, DH], BF16, tag="flip")
            for t in range(PACK):
                nc.tensor.transpose(wc_flip[:, t, :], wc_raw[:, n, t * P : (t + 1) * P], ident_bf[:])
            nc.scalar.copy(out=wc_grouped[:, n], in_=wc_flip[:].rearrange("p t k -> p k t"))

        xhat_flip = flip_psum.tile([P, PACK, P], F32, tag="flip")
        for t in range(PACK):
            nc.tensor.transpose(xhat_flip[:, t, :], xhat[:, t * P : (t + 1) * P], ident_f32[:])
        xn_grouped = keep.tile([P, P, PACK], BF16, align_bytes=64)
        for t in range(PACK):
            nc.vector.tensor_scalar(
                out=xn_grouped[:, :, t], in0=xhat_flip[:, t, :],
                scalar1=gain[:, t : t + 1], scalar2=shift[:, t : t + 1], op0=ALU.mult, op1=ALU.add,
            )
        xn_codes = keep.tile([P, P], U32, align_bytes=64)
        xn_scales = keep.tile([P, P], U8, align_bytes=64)
        nc.vector.quantize_mx(
            out=xn_codes[:].bitcast(FP8X4), scales=xn_scales[:],
            in_=xn_grouped[:].rearrange("p r t -> p (r t)"),
        )
        wc_codes = keep.tile([P, HEADS * DH], U32, align_bytes=64)
        wc_scales = keep.tile([P, HEADS * DH], U8, align_bytes=64)
        nc.vector.quantize_mx(
            out=wc_codes[:].bitcast(FP8X4), scales=wc_scales[:],
            in_=wc_grouped[:].rearrange("p n k t -> p (n k t)"),
        )

        grouped_tiles = {}
        mx_tiles = {}
        result_tiles = {}

        def flip_pass(s):
            raw = raw_tiles[s // PASSES_PER_CHUNK]
            first_m = (s % PASSES_PER_CHUNK) * PASS_M
            grouped = grouped_pool.tile([P, PASS_M * P], BF16, align_bytes=64)
            for b in range(PASS_M // BANK_T):
                flip = flip_psum.tile([P, BANK_T * P], BF16, tag="flip")
                for q in range(BANK_T):
                    m = first_m + b * BANK_T + q
                    nc.tensor.transpose(flip[:, q * P : (q + 1) * P], raw[:, m * DH : (m + 1) * DH], ident_bf[:])
                nc.scalar.copy(
                    out=grouped[:, b * BANK_T * P : (b + 1) * BANK_T * P].bitcast(F32), in_=flip[:].bitcast(F32)
                )
            grouped_tiles[s] = grouped

        def quantise_pass(s):
            codes = mx_pool.tile([P, PASS_COLS], U32, align_bytes=64)
            scales = mx_pool.tile([P, PASS_COLS], U8, align_bytes=64)
            nc.vector.quantize_mx(out=codes[:].bitcast(FP8X4), scales=scales[:], in_=grouped_tiles[s][:])
            mx_tiles[s] = (codes, scales)

        def multiply_pass(s):
            codes, scales = mx_tiles[s]
            sums = sum_psum.tile([P, PASS_COLS], F32, tag="sums")
            nc.tensor.matmul_mx(
                out=sums[:], lhsT=c_codes[:].bitcast(FP8X4), lhsT_scale=c_scales[:],
                rhs=codes[:].bitcast(FP8X4), rhs_scale=scales[:], start=True, stop=True,
            )
            c, half = divmod(s, PASSES_PER_CHUNK)
            if half == 0:
                result = result_pool.tile([P, CHUNK_COLS], F32)
                result_tiles[c] = result
            result = result_tiles[c]
            nc.vector.tensor_copy(
                out=result[:].rearrange(
                    "r (g h a b) -> r h a g b", g=GROUPS, h=PASSES_PER_CHUNK, b=LINE_F32
                )[:, half],
                in_=sums[:].rearrange("r (a b g) -> r a g b", b=LINE_F32, g=GROUPS),
            )
            if half == PASSES_PER_CHUNK - 1:
                nc.sync.dma_start(out=out_cols[:, c * CHUNK_COLS : (c + 1) * CHUNK_COLS], in_=result[:])

        def flip_round(i):
            for s in range(i * ROUND, (i + 1) * ROUND):
                flip_pass(s)

        def quantise_round(i):
            for s in range(i * ROUND, (i + 1) * ROUND):
                quantise_pass(s)

        def multiply_round(i):
            for s in range(i * ROUND, (i + 1) * ROUND):
                multiply_pass(s)

        raise_clock(WAIT_FOR_W_K)
        flip_round(0)
        c_sums = sum_psum.tile([P, HEADS, P], F32, tag="sums")
        for n in range(HEADS):
            nc.tensor.matmul_mx(
                out=c_sums[:, n, :],
                lhsT=wc_codes[:, n * DH : (n + 1) * DH].bitcast(FP8X4),
                lhsT_scale=wc_scales[:, n * DH : (n + 1) * DH],
                rhs=xn_codes[:].bitcast(FP8X4), rhs_scale=xn_scales[:], start=True, stop=True,
            )
        quantise_round(0)
        c_grouped = keep.tile([P, P, HEADS], BF16, align_bytes=64)
        for n in range(HEADS):
            nc.vector.tensor_scalar(
                out=c_grouped[:, :, n], in0=c_sums[:, n, :],
                scalar1=bias[:, n : n + 1], scalar2=None, op0=ALU.add,
            )
        c_codes = keep.tile([P, P], U32, align_bytes=64)
        c_scales = keep.tile([P, P], U8, align_bytes=64)
        nc.vector.quantize_mx(
            out=c_codes[:].bitcast(FP8X4), scales=c_scales[:],
            in_=c_grouped[:].rearrange("k r n -> k (r n)"),
        )

        rounds = PASSES // ROUND
        for i in range(1, rounds):
            flip_round(i)
            quantise_round(i)
            multiply_round(i - 1)
        multiply_round(rounds - 1)
